import numpy as np
import ml_dtypes


def mxq(x, axis, fmt="e4m3"):
    dtype, down = {"e4m3": (ml_dtypes.float8_e4m3fn, 7), "e5m2": (ml_dtypes.float8_e5m2, 14)}[fmt]
    v = np.moveaxis(np.asarray(x, np.float32).astype(ml_dtypes.bfloat16).astype(np.float64), axis, -1)
    blocks = v.reshape(v.shape[:-1] + (-1, 32))
    amax = np.abs(blocks).max(-1, keepdims=True)
    byte = np.maximum(np.where(amax > 0, np.frexp(amax)[1] - 1 + 127, 0) - down, 1)
    scale = np.exp2(byte - 127.0)
    codes = (blocks / scale).astype(np.float32).astype(dtype).astype(np.float64)
    return np.moveaxis((codes * scale).reshape(v.shape), -1, axis)


WIDE = False


def mx_kscale(k):
    if not WIDE:
        return np.ones(k)
    levels = np.array([10, -10, 5, -5, 0])
    a = np.random.permutation(np.resize(levels, k // 512 * 4)).reshape(k // 512, 4)
    idx = np.arange(k)
    return np.exp2(a[idx // 512, idx % 128 // 32])


BF16 = ml_dtypes.bfloat16


def bf(x):
    return np.asarray(x, np.float32).astype(BF16)


def f64(x):
    return np.asarray(x).astype(np.float64)


B, T, N, C, WIN, F = 1, 4, 512, 512, 3, 3
NW = T - WIN + 1


def sigmoid(v):
    return 1.0 / (1.0 + np.exp(-v))


def setup_inputs():
    t = mx_kscale(C)
    return {"agg": bf(np.random.standard_normal((B, NW, N, C)) * t),
            "W": bf(np.random.standard_normal((NW, F, C, 2 * C)) / np.sqrt(C) / t[:, None]),
            "b": bf(np.random.standard_normal((NW, F, 2 * C)) * 0.3)}


def reference(agg, W, b):
    pre = (mxq(f64(agg), 3, "e4m3")[:, :, None] @ mxq(f64(W), 2, "e4m3")) + f64(b)[None, :, :, None, :]
    lhs, rhs = pre[..., :C], pre[..., C:]
    glu = lhs * sigmoid(rhs)
    return glu.max(axis=2)

@@ -1,0 +1,236 @@
+from contextlib import ExitStack
+
+import concourse.mybir as mybir
+from concourse.masks import make_identity
+
+F32 = mybir.dt.float32
+BF16 = mybir.dt.bfloat16
+U32 = mybir.dt.uint32
+U8 = mybir.dt.uint8
+FP8X4 = mybir.dt.float8_e4m3fn_x4
+ACT = mybir.ActivationFunctionType
+ALU = mybir.AluOpType
+
+P = 128
+NW = 2
+NF = 3
+NODES = 512
+CH = 512
+UNITS = NW * NF
+STEPS = UNITS * 4
+PIECE = 256
+PIECE_COL = (0, 512, 256, 768)
+FLOPS = 2 * NW * NF * NODES * 512 * 2 * CH
+
+PINNED = True
+LOOK = 5
+ASSIGN = "VSVSVSVVSSVSSSVVVSVSVSSS"
+
+
+def tile_stsindividuallayer_pb_kernel(tc, agg, W, b, out):
+    nc = tc.nc
+    with ExitStack() as ctx:
+        const = ctx.enter_context(tc.tile_pool(name="const", bufs=1))
+        keep = ctx.enter_context(tc.tile_pool(name="keep", bufs=1))
+        stage = ctx.enter_context(tc.tile_pool(name="stage", bufs=4))
+        work = ctx.enter_context(tc.tile_pool(name="work", bufs=3))
+        psum_mx = ctx.enter_context(tc.psum_pool(name="psum_mx", bufs=3))
+        psum_tr = ctx.enter_context(tc.psum_pool(name="psum_tr", bufs=2))
+        if PINNED:
+            ctx.enter_context(tc.manual_schedule())
+
+        raw = [keep.tile([P, 4, 2 * CH], BF16, name="raw%d" % u) for u in range(UNITS)]
+        wcodes = [keep.tile([P, 2 * CH], U32, name="wcodes%d" % u, align_bytes=64) for u in range(UNITS)]
+        wscales = [keep.tile([P, 2 * CH], U8, name="wscales%d" % u, align_bytes=64) for u in range(UNITS)]
+        x = [keep.tile([P, 4, 512], BF16, name="x%d" % w) for w in range(NW)]
+        xg = [keep.tile([P, 4 * NODES], BF16, name="xg%d" % w, align_bytes=64) for w in range(NW)]
+        xcodes = [keep.tile([P, NODES], U32, name="xcodes%d" % w, align_bytes=64) for w in range(NW)]
+        xscales = [keep.tile([P, NODES], U8, name="xscales%d" % w, align_bytes=64) for w in range(NW)]
+        acc = [keep.tile([P, 4, NODES], F32, name="acc%d" % w) for w in range(NW)]
+
+        ident_f = const.tile([P, P], F32, name="ident_f")
+        ident_b = const.tile([P, P], BF16, name="ident_b")
+        braw = const.tile([P, P], BF16, name="braw")
+        bias = const.tile([P, UNITS * 8], F32, name="bias")
+        warm = const.tile([P, 2], F32, name="warm")
+
+        nc.vector.memset(warm[:], 0.0)
+        nc.vector.memset(braw[:], 0.0)
+        nc.scalar.dma_start(out=braw[0 : UNITS * 8, :], in_=b.rearrange("w f (c p) -> (w f c) p", p=P))
+        nc.scalar.activation(out=warm[:, 1:2], in_=warm[:, 0:1], func=ACT.Sigmoid)
+        make_identity(nc, ident_f[:])
+        make_identity(nc, ident_b[:])
+
+        def wview(u):
+            return W[u // NF, u % NF].rearrange("(p j) n -> p j n", j=4)
+
+        def load_w(u, c0, c1):
+            nc.sync.dma_start(out=raw[u][:, :, c0:c1], in_=wview(u)[:, :, c0:c1])
+
+        def load_x(w, i0, i1):
+            nc.sync.dma_start(out=x[w][:, i0:i1, :], in_=agg[0, w].rearrange("(p i) k -> p i k", i=4)[:, i0:i1, :])
+
+        load_x(0, 0, 2)
+        load_x(0, 2, 4)
+        for q in range(4):
+            load_w(0, PIECE_COL[q], PIECE_COL[q] + PIECE)
+        load_w(1, 0, CH)
+        load_w(1, CH, 2 * CH)
+        load_w(2, 0, 2 * CH)
+        load_x(1, 0, 4)
+        for u in range(3, UNITS):
+            load_w(u, 0, 2 * CH)
+
+        grouped = {}
+        banks = {}
+        sigs = {}
+        gs = {}
+        trs = {}
+
+        def copy_on(eng, dst, src):
+            if eng == "V":
+                nc.vector.tensor_copy(out=dst, in_=src)
+            else:
+                nc.scalar.copy(out=dst, in_=src)
+
+        def regroup(m):
+            u, q = divmod(m, 4)
+            c0 = PIECE_COL[q]
+            gt = stage.tile([P, PIECE, 4], BF16, name="grouped", align_bytes=64)
+            grouped[m] = gt
+            copy_on(
+                ASSIGN[m],
+                gt[:].rearrange("p (c i) t -> p c t i", i=4),
+                raw[u][:, :, c0 : c0 + PIECE].rearrange("p t (c i) -> p c t i", i=4),
+            )
+
+        def quant(m):
+            u, q = divmod(m, 4)
+            c0 = PIECE_COL[q]
+            nc.vector.quantize_mx(
+                out=wcodes[u][:, c0 : c0 + PIECE].bitcast(FP8X4),
+                scales=wscales[u][:, c0 : c0 + PIECE],
+                in_=grouped[m][:].rearrange("p c t -> p (c t)"),
+            )
+
+        def agg_tr(w, h):
+            xt = psum_tr.tile([P, 2, 256], F32, name="xt", tag="tr")
+            trs[("x", w, h)] = xt
+            for ii in range(2):
+                words = x[w][:, 2 * h + ii, :].bitcast(F32).rearrange("p (m s) -> p s m", s=2)
+                for s in range(2):
+                    nc.tensor.transpose(xt[:, s, P * ii : P * ii + P], words[:, s, :], ident_f[:])
+
+        def agg_ev(w, h, eng):
+            dst = xg[w][:].bitcast(F32).rearrange("p (r s) -> p r s", s=2)[:, 256 * h : 256 * h + 256, :]
+            copy_on(eng, dst, trs[("x", w, h)][:].rearrange("p s r -> p r s"))
+
+        def agg_q(w):
+            nc.vector.quantize_mx(out=xcodes[w][:].bitcast(FP8X4), scales=xscales[w][:], in_=xg[w][:])
+
+        def mx(k):
+            u, c = divmod(k, 4)
+            w = u // NF
+            pr = psum_mx.tile([P, NODES], F32, name="pr", tag="rhs")
+            pl = psum_mx.tile([P, NODES], F32, name="pl", tag="lhs")
+            banks[k] = (pl, pr)
+            for bank, c0 in ((pr, CH + P * c), (pl, P * c)):
+                nc.tensor.matmul_mx(
+                    out=bank[:],
+                    lhsT=wcodes[u][:, c0 : c0 + P].bitcast(FP8X4),
+                    lhsT_scale=wscales[u][:, c0 : c0 + P],
+                    rhs=xcodes[w][:].bitcast(FP8X4),
+                    rhs_scale=xscales[w][:],
+                    start=True,
+                    stop=True,
+                )
+
+        def sig(k):
+            u, c = divmod(k, 4)
+            st = work.tile([P, NODES], F32, name="sig")
+            sigs[k] = st
+            col = u * 8 + 4 + c
+            nc.scalar.activation(out=st[:], in_=banks[k][1][:], func=ACT.Sigmoid, bias=bias[:, col : col + 1], scale=1.0)
+
+        def stt(k):
+            u, c = divmod(k, 4)
+            w, f = divmod(u, NF)
+            if f == 0:
+                dst = acc[w][:, c, :]
+            else:
+                gt = work.tile([P, NODES], F32, name="glu")
+                gs[k] = gt
+                dst = gt[:]
+            col = u * 8 + c
+            nc.vector.scalar_tensor_tensor(
+                out=dst, in0=banks[k][0][:], scalar=bias[:, col : col + 1], in1=sigs[k][:], op0=ALU.add, op1=ALU.mult
+            )
+
+        def vmax(k):
+            u, c = divmod(k, 4)
+            w, f = divmod(u, NF)
+            if f > 0:
+                nc.vector.tensor_tensor(out=acc[w][:, c, :], in0=acc[w][:, c, :], in1=gs[k][:], op=ALU.max)
+
+        def last_branch(k):
+            return 0 <= k < STEPS and (k // 4) % NF == NF - 1
+
+        def out_tr(k):
+            u, c = divmod(k, 4)
+            w = u // NF
+            pt = psum_tr.tile([P, 4, P], F32, name="pt", tag="tr")
+            trs[k] = pt
+            for i in range(4):
+                nc.tensor.transpose(pt[:, i, :], acc[w][:, c, P * i : P * i + P], ident_f[:])
+
+        def out_ev(k):
+            u, c = divmod(k, 4)
+            w = u // NF
+            res = work.tile([P, 4, P], F32, name="res")
+            nc.scalar.copy(out=res[:], in_=trs[k][:])
+            nc.sync.dma_start(
+                out=out[0, w].rearrange("(p i) c -> p i c", i=4)[:, :, P * c : P * c + P], in_=res[:]
+            )
+
+        bt = psum_tr.tile([P, P], BF16, name="bt", tag="tr")
+        nc.tensor.transpose(bt[:], braw[:], ident_b[:])
+        nc.vector.tensor_copy(out=bias[:], in_=bt[:, 0 : UNITS * 8])
+        agg_tr(0, 0)
+        agg_tr(0, 1)
+        agg_ev(0, 0, "V")
+        regroup(0)
+        agg_ev(0, 1, "V")
+        regroup(1)
+        agg_q(0)
+        quant(0)
+        quant(1)
+        regroup(2)
+        regroup(3)
+
+        for j in range(-2, STEPS + 4):
+            if 0 <= j + 2 < STEPS:
+                mx(j + 2)
+            if last_branch(j - 2):
+                out_tr(j - 2)
+            if j == 4 or j == 5:
+                agg_tr(1, j - 4)
+            if 0 <= j + 1 < STEPS:
+                sig(j + 1)
+            if 0 <= j < STEPS:
+                stt(j)
+            if 0 <= j - 1 < STEPS:
+                vmax(j - 1)
+            m = j + LOOK
+            if j == -2:
+                quant(2)
+                quant(3)
+            if 4 <= m - 1 < 4 * UNITS:
+                quant(m - 1)
+            if 4 <= m < 4 * UNITS:
+                regroup(m)
+            if last_branch(j - 3):
+                out_ev(j - 3)
+            if j == 5 or j == 6:
+                agg_ev(1, j - 5, "S")
+            if j == 7:
+                agg_q(1)

@@ -24,7 +24,7 @@ FLOPS = 2 * NW * NF * NODES * 512 * 2 * CH
 
 PINNED = True
 LOOK = 5
-ASSIGN = "VSVSVSVVSSVSSSVVVSVSVSSS"
+ASSIGN = "VSVSVVSSVSSSSSSSVVVSSSSS"
 
 
 def tile_stsindividuallayer_pb_kernel(tc, agg, W, b, out):

@@ -18,13 +18,13 @@ NODES = 512
 CH = 512
 UNITS = NW * NF
 STEPS = UNITS * 4
-PIECE = 256
-PIECE_COL = (0, 512, 256, 768)
+PAIRS = STEPS // 2
 FLOPS = 2 * NW * NF * NODES * 512 * 2 * CH
 
-PINNED = True
-LOOK = 5
-ASSIGN = "VSVSVVSSVSSSSSSSVVVSSSSS"
+PART = {"r0": (512, 256), "r1": (768, 256), "l0": (0, 256), "g2": (256, 128), "g3": (384, 128)}
+ON_VECTOR = ((0, "l0"), (1, "r0"), (1, "r1"), (2, "l0"), (5, "l0"))
+USE_G = True
+LATE = [9, 10]
 
 
 def tile_stsindividuallayer_pb_kernel(tc, agg, W, b, out):
@@ -32,12 +32,12 @@ def tile_stsindividuallayer_pb_kernel(tc, agg, W, b, out):
     with ExitStack() as ctx:
         const = ctx.enter_context(tc.tile_pool(name="const", bufs=1))
         keep = ctx.enter_context(tc.tile_pool(name="keep", bufs=1))
-        stage = ctx.enter_context(tc.tile_pool(name="stage", bufs=4))
+        stage = ctx.enter_context(tc.tile_pool(name="stage", bufs=6))
         work = ctx.enter_context(tc.tile_pool(name="work", bufs=3))
-        psum_mx = ctx.enter_context(tc.psum_pool(name="psum_mx", bufs=3))
+        psum_l = ctx.enter_context(tc.psum_pool(name="psum_l", bufs=4))
+        psum_r = ctx.enter_context(tc.psum_pool(name="psum_r", bufs=2))
         psum_tr = ctx.enter_context(tc.psum_pool(name="psum_tr", bufs=2))
-        if PINNED:
-            ctx.enter_context(tc.manual_schedule())
+        ctx.enter_context(tc.manual_schedule())
 
         raw = [keep.tile([P, 4, 2 * CH], BF16, name="raw%d" % u) for u in range(UNITS)]
         wcodes = [keep.tile([P, 2 * CH], U32, name="wcodes%d" % u, align_bytes=64) for u in range(UNITS)]
@@ -61,19 +61,19 @@ def tile_stsindividuallayer_pb_kernel(tc, agg, W, b, out):
         make_identity(nc, ident_f[:])
         make_identity(nc, ident_b[:])
 
-        def wview(u):
-            return W[u // NF, u % NF].rearrange("(p j) n -> p j n", j=4)
-
         def load_w(u, c0, c1):
-            nc.sync.dma_start(out=raw[u][:, :, c0:c1], in_=wview(u)[:, :, c0:c1])
+            view = W[u // NF, u % NF].rearrange("(p j) n -> p j n", j=4)
+            nc.sync.dma_start(out=raw[u][:, :, c0:c1], in_=view[:, :, c0:c1])
 
         def load_x(w, i0, i1):
             nc.sync.dma_start(out=x[w][:, i0:i1, :], in_=agg[0, w].rearrange("(p i) k -> p i k", i=4)[:, i0:i1, :])
 
         load_x(0, 0, 2)
         load_x(0, 2, 4)
-        for q in range(4):
-            load_w(0, PIECE_COL[q], PIECE_COL[q] + PIECE)
+        load_w(0, 512, 768)
+        load_w(0, 0, 256)
+        load_w(0, 768, 1024)
+        load_w(0, 256, 512)
         load_w(1, 0, CH)
         load_w(1, CH, 2 * CH)
         load_w(2, 0, 2 * CH)
@@ -82,7 +82,8 @@ def tile_stsindividuallayer_pb_kernel(tc, agg, W, b, out):
             load_w(u, 0, 2 * CH)
 
         grouped = {}
-        banks = {}
+        lbank = {}
+        rbank = {}
         sigs = {}
         gs = {}
         trs = {}
@@ -93,24 +94,45 @@ def tile_stsindividuallayer_pb_kernel(tc, agg, W, b, out):
             else:
                 nc.scalar.copy(out=dst, in_=src)
 
-        def regroup(m):
-            u, q = divmod(m, 4)
-            c0 = PIECE_COL[q]
-            gt = stage.tile([P, PIECE, 4], BF16, name="grouped", align_bytes=64)
-            grouped[m] = gt
-            copy_on(
-                ASSIGN[m],
-                gt[:].rearrange("p (c i) t -> p c t i", i=4),
-                raw[u][:, :, c0 : c0 + PIECE].rearrange("p t (c i) -> p c t i", i=4),
-            )
+        def engine_of(u, name):
+            if name in ("g2", "g3"):
+                return "G" if (USE_G and u > 0) else "V"
+            return "V" if (u, name) in ON_VECTOR else "S"
 
-        def quant(m):
-            u, q = divmod(m, 4)
-            c0 = PIECE_COL[q]
+        def regroup(u, name):
+            if u >= UNITS:
+                return
+            c0, n = PART[name]
+            if name in ("g2", "g3"):
+                gt = stage.tile([P, n, 4], BF16, name="late", bufs=1, align_bytes=64)
+            else:
+                gt = stage.tile([P, n, 4], BF16, name="grouped", align_bytes=64)
+            grouped[(u, name)] = gt
+            eng = engine_of(u, name)
+            if eng == "G":
+                nc.gpsimd.tensor_scalar(
+                    out=gt[:],
+                    in0=raw[u][:, :, c0 : c0 + n].rearrange("p t c -> p c t"),
+                    scalar1=1.0,
+                    scalar2=0.0,
+                    op0=ALU.mult,
+                    op1=ALU.add,
+                )
+            else:
+                copy_on(
+                    eng,
+                    gt[:].rearrange("p (c i) t -> p c t i", i=4),
+                    raw[u][:, :, c0 : c0 + n].rearrange("p t (c i) -> p c t i", i=4),
+                )
+
+        def quant(u, name):
+            if u >= UNITS:
+                return
+            c0, n = PART[name]
             nc.vector.quantize_mx(
-                out=wcodes[u][:, c0 : c0 + PIECE].bitcast(FP8X4),
-                scales=wscales[u][:, c0 : c0 + PIECE],
-                in_=grouped[m][:].rearrange("p c t -> p (c t)"),
+                out=wcodes[u][:, c0 : c0 + n].bitcast(FP8X4),
+                scales=wscales[u][:, c0 : c0 + n],
+                in_=grouped[(u, name)][:].rearrange("p c t -> p (c t)"),
             )
 
         def agg_tr(w, h):
@@ -128,29 +150,40 @@ def tile_stsindividuallayer_pb_kernel(tc, agg, W, b, out):
         def agg_q(w):
             nc.vector.quantize_mx(out=xcodes[w][:].bitcast(FP8X4), scales=xscales[w][:], in_=xg[w][:])
 
-        def mx(k):
-            u, c = divmod(k, 4)
+        def one_pass(bank, u, c0):
             w = u // NF
-            pr = psum_mx.tile([P, NODES], F32, name="pr", tag="rhs")
-            pl = psum_mx.tile([P, NODES], F32, name="pl", tag="lhs")
-            banks[k] = (pl, pr)
-            for bank, c0 in ((pr, CH + P * c), (pl, P * c)):
-                nc.tensor.matmul_mx(
-                    out=bank[:],
-                    lhsT=wcodes[u][:, c0 : c0 + P].bitcast(FP8X4),
-                    lhsT_scale=wscales[u][:, c0 : c0 + P],
-                    rhs=xcodes[w][:].bitcast(FP8X4),
-                    rhs_scale=xscales[w][:],
-                    start=True,
-                    stop=True,
-                )
+            nc.tensor.matmul_mx(
+                out=bank[:],
+                lhsT=wcodes[u][:, c0 : c0 + P].bitcast(FP8X4),
+                lhsT_scale=wscales[u][:, c0 : c0 + P],
+                rhs=xcodes[w][:].bitcast(FP8X4),
+                rhs_scale=xscales[w][:],
+                start=True,
+                stop=True,
+            )
+
+        def passr(k):
+            if k >= STEPS:
+                return
+            u, c = divmod(k, 4)
+            rbank[k] = psum_r.tile([P, NODES], F32, name="pr")
+            one_pass(rbank[k], u, CH + P * c)
+
+        def passl(k):
+            if k >= STEPS:
+                return
+            u, c = divmod(k, 4)
+            lbank[k] = psum_l.tile([P, NODES], F32, name="pl")
+            one_pass(lbank[k], u, P * c)
 
         def sig(k):
+            if k >= STEPS:
+                return
             u, c = divmod(k, 4)
-            st = work.tile([P, NODES], F32, name="sig")
+            st = work.tile([P, NODES], F32, name="sig", bufs=5)
             sigs[k] = st
             col = u * 8 + 4 + c
-            nc.scalar.activation(out=st[:], in_=banks[k][1][:], func=ACT.Sigmoid, bias=bias[:, col : col + 1], scale=1.0)
+            nc.scalar.activation(out=st[:], in_=rbank[k][:], func=ACT.Sigmoid, bias=bias[:, col : col + 1], scale=1.0)
 
         def stt(k):
             u, c = divmod(k, 4)
@@ -158,22 +191,28 @@ def tile_stsindividuallayer_pb_kernel(tc, agg, W, b, out):
             if f == 0:
                 dst = acc[w][:, c, :]
             else:
-                gt = work.tile([P, NODES], F32, name="glu")
-                gs[k] = gt
-                dst = gt[:]
+                if c % 2 == 0:
+                    gs[k] = work.tile([P, 2, NODES], F32, name="glu2")
+                dst = gs[k // 2 * 2][:, c % 2, :]
             col = u * 8 + c
             nc.vector.scalar_tensor_tensor(
-                out=dst, in0=banks[k][0][:], scalar=bias[:, col : col + 1], in1=sigs[k][:], op0=ALU.add, op1=ALU.mult
+                out=dst, in0=lbank[k][:], scalar=bias[:, col : col + 1], in1=sigs[k][:], op0=ALU.add, op1=ALU.mult
             )
 
-        def vmax(k):
+        def max_pair(d):
+            k = 2 * d
             u, c = divmod(k, 4)
             w, f = divmod(u, NF)
-            if f > 0:
-                nc.vector.tensor_tensor(out=acc[w][:, c, :], in0=acc[w][:, c, :], in1=gs[k][:], op=ALU.max)
+            if d >= 0 and f > 0:
+                pair = acc[w][:, c : c + 2, :]
+                nc.vector.tensor_tensor(out=pair, in0=pair, in1=gs[k][:], op=ALU.max)
 
-        def last_branch(k):
-            return 0 <= k < STEPS and (k // 4) % NF == NF - 1
+        def max_one(k):
+            u, c = divmod(k, 4)
+            w = u // NF
+            nc.vector.tensor_tensor(
+                out=acc[w][:, c, :], in0=acc[w][:, c, :], in1=gs[k // 2 * 2][:, c % 2, :], op=ALU.max
+            )
 
         def out_tr(k):
             u, c = divmod(k, 4)
@@ -198,39 +237,83 @@ def tile_stsindividuallayer_pb_kernel(tc, agg, W, b, out):
         agg_tr(0, 0)
         agg_tr(0, 1)
         agg_ev(0, 0, "V")
-        regroup(0)
+        regroup(0, "r0")
+        regroup(0, "l0")
         agg_ev(0, 1, "V")
-        regroup(1)
         agg_q(0)
-        quant(0)
-        quant(1)
-        regroup(2)
-        regroup(3)
+        quant(0, "r0")
+        quant(0, "l0")
+        passr(0)
+        passr(1)
+        passl(0)
+        passl(1)
+        regroup(0, "r1")
+        regroup(0, "g2")
+        sig(0)
+        sig(1)
+        quant(0, "r1")
+        quant(0, "g2")
+        regroup(0, "g3")
+        passr(2)
+        passr(3)
+        passl(2)
+        regroup(1, "r0")
+        regroup(1, "l0")
+        quant(0, "g3")
+        passl(3)
+        regroup(1, "g2")
 
-        for j in range(-2, STEPS + 4):
-            if 0 <= j + 2 < STEPS:
-                mx(j + 2)
-            if last_branch(j - 2):
-                out_tr(j - 2)
-            if j == 4 or j == 5:
-                agg_tr(1, j - 4)
-            if 0 <= j + 1 < STEPS:
-                sig(j + 1)
-            if 0 <= j < STEPS:
-                stt(j)
-            if 0 <= j - 1 < STEPS:
-                vmax(j - 1)
-            m = j + LOOK
-            if j == -2:
-                quant(2)
-                quant(3)
-            if 4 <= m - 1 < 4 * UNITS:
-                quant(m - 1)
-            if 4 <= m < 4 * UNITS:
-                regroup(m)
-            if last_branch(j - 3):
-                out_ev(j - 3)
-            if j == 5 or j == 6:
-                agg_ev(1, j - 5, "S")
-            if j == 7:
+        for d in range(PAIRS):
+            u_next = d // 2 + 1
+            fine = d >= PAIRS - 1
+            if d == 2:
+                agg_tr(1, 0)
+                agg_tr(1, 1)
+            if d in LATE:
+                out_tr(8 + 2 * LATE.index(d))
+                out_tr(9 + 2 * LATE.index(d))
+            sig(2 * d + 2)
+            sig(2 * d + 3)
+            if not fine:
+                stt(2 * d)
+                stt(2 * d + 1)
+                max_pair(d - 1)
+            else:
+                stt(2 * d)
+                max_one(2 * d - 2)
+                out_tr(2 * d - 2)
+                stt(2 * d + 1)
+                max_one(2 * d - 1)
+                out_ev(2 * d - 2)
+                out_tr(2 * d - 1)
+                max_one(2 * d)
+                out_ev(2 * d - 1)
+                out_tr(2 * d)
+                max_one(2 * d + 1)
+                out_ev(2 * d)
+                out_tr(2 * d + 1)
+                out_ev(2 * d + 1)
+            if d == 2:
+                agg_ev(1, 0, "S")
+                agg_ev(1, 1, "S")
+            if d == 3:
                 agg_q(1)
+            if d % 2 == 0:
+                quant(u_next, "r0")
+                quant(u_next, "l0")
+                regroup(u_next, "r1")
+                quant(u_next, "g2")
+                regroup(u_next, "g3")
+            else:
+                quant(u_next, "r1")
+                regroup(u_next + 1, "r0")
+                regroup(u_next + 1, "l0")
+                quant(u_next, "g3")
+                regroup(u_next + 1, "g2")
+            passr(2 * d + 4)
+            passr(2 * d + 5)
+            passl(2 * d + 4)
+            passl(2 * d + 5)
+            if d in LATE:
+                out_ev(8 + 2 * LATE.index(d))
+                out_ev(9 + 2 * LATE.index(d))

@@ -22,7 +22,7 @@ PAIRS = STEPS // 2
 FLOPS = 2 * NW * NF * NODES * 512 * 2 * CH
 
 PART = {"r0": (512, 256), "r1": (768, 256), "l0": (0, 256), "g2": (256, 128), "g3": (384, 128)}
-ON_VECTOR = ((0, "l0"), (1, "r0"), (1, "r1"), (2, "l0"), (5, "l0"))
+ON_VECTOR = ((0, "r0"), (0, "l0"), (1, "r0"), (1, "r1"), (2, "l0"), (5, "l0"))
 USE_G = True
 LATE = [9, 10]
 
@@ -70,12 +70,8 @@ def tile_stsindividuallayer_pb_kernel(tc, agg, W, b, out):
 
         load_x(0, 0, 2)
         load_x(0, 2, 4)
-        load_w(0, 512, 768)
-        load_w(0, 0, 256)
-        load_w(0, 768, 1024)
-        load_w(0, 256, 512)
-        load_w(1, 0, CH)
-        load_w(1, CH, 2 * CH)
+        load_w(0, 0, 2 * CH)
+        load_w(1, 0, 2 * CH)
         load_w(2, 0, 2 * CH)
         load_x(1, 0, 4)
         for u in range(3, UNITS):
@@ -237,18 +233,18 @@ def tile_stsindividuallayer_pb_kernel(tc, agg, W, b, out):
         agg_tr(0, 0)
         agg_tr(0, 1)
         agg_ev(0, 0, "V")
-        regroup(0, "r0")
-        regroup(0, "l0")
         agg_ev(0, 1, "V")
         agg_q(0)
+        regroup(0, "r0")
+        regroup(0, "l0")
+        regroup(0, "r1")
         quant(0, "r0")
+        regroup(0, "g2")
         quant(0, "l0")
         passr(0)
         passr(1)
         passl(0)
         passl(1)
-        regroup(0, "r1")
-        regroup(0, "g2")
         sig(0)
         sig(1)
         quant(0, "r1")

@@ -22,9 +22,9 @@ PAIRS = STEPS // 2
 FLOPS = 2 * NW * NF * NODES * 512 * 2 * CH
 
 PART = {"r0": (512, 256), "r1": (768, 256), "l0": (0, 256), "g2": (256, 128), "g3": (384, 128)}
-ON_VECTOR = ((0, "r0"), (0, "l0"), (1, "r0"), (1, "r1"), (2, "l0"), (5, "l0"))
+ON_VECTOR = ((0, "l0"), (1, "r0"), (1, "r1"), (2, "l0"), (5, "l0"))
 USE_G = True
-LATE = [9, 10]
+LATE = [8, 9]
 
 
 def tile_stsindividuallayer_pb_kernel(tc, agg, W, b, out):
@@ -47,6 +47,7 @@ def tile_stsindividuallayer_pb_kernel(tc, agg, W, b, out):
         xcodes = [keep.tile([P, NODES], U32, name="xcodes%d" % w, align_bytes=64) for w in range(NW)]
         xscales = [keep.tile([P, NODES], U8, name="xscales%d" % w, align_bytes=64) for w in range(NW)]
         acc = [keep.tile([P, 4, NODES], F32, name="acc%d" % w) for w in range(NW)]
+        acc_t = keep.tile([P, 4, CH], F32, name="acc_t")
 
         ident_f = const.tile([P, P], F32, name="ident_f")
         ident_b = const.tile([P, P], BF16, name="ident_b")
@@ -70,8 +71,12 @@ def tile_stsindividuallayer_pb_kernel(tc, agg, W, b, out):
 
         load_x(0, 0, 2)
         load_x(0, 2, 4)
-        load_w(0, 0, 2 * CH)
-        load_w(1, 0, 2 * CH)
+        load_w(0, 512, 768)
+        load_w(0, 0, 256)
+        load_w(0, 768, 1024)
+        load_w(0, 256, 512)
+        load_w(1, 0, CH)
+        load_w(1, CH, 2 * CH)
         load_w(2, 0, 2 * CH)
         load_x(1, 0, 4)
         for u in range(3, UNITS):
@@ -203,13 +208,6 @@ def tile_stsindividuallayer_pb_kernel(tc, agg, W, b, out):
                 pair = acc[w][:, c : c + 2, :]
                 nc.vector.tensor_tensor(out=pair, in0=pair, in1=gs[k][:], op=ALU.max)
 
-        def max_one(k):
-            u, c = divmod(k, 4)
-            w = u // NF
-            nc.vector.tensor_tensor(
-                out=acc[w][:, c, :], in0=acc[w][:, c, :], in1=gs[k // 2 * 2][:, c % 2, :], op=ALU.max
-            )
-
         def out_tr(k):
             u, c = divmod(k, 4)
             w = u // NF
@@ -227,24 +225,53 @@ def tile_stsindividuallayer_pb_kernel(tc, agg, W, b, out):
                 out=out[0, w].rearrange("(p i) c -> p i c", i=4)[:, :, P * c : P * c + P], in_=res[:]
             )
 
-        bt = psum_tr.tile([P, P], BF16, name="bt", tag="tr")
-        nc.tensor.transpose(bt[:], braw[:], ident_b[:])
-        nc.vector.tensor_copy(out=bias[:], in_=bt[:, 0 : UNITS * 8])
+        def bank_for_transposes(pool):
+            if pool == "tr":
+                return psum_tr.tile([P, 4, P], F32, name="pt", tag="tr")
+            return psum_r.tile([P, 4, P], F32, name="pr")
+
+        def acc_tr(c, pool):
+            pt = bank_for_transposes(pool)
+            trs[("a", c)] = pt
+            for i in range(4):
+                nc.tensor.transpose(pt[:, i, :], acc[1][:, c, P * i : P * i + P], ident_f[:])
+
+        def acc_ev(c):
+            nc.scalar.copy(out=acc_t[:, :, P * c : P * c + P], in_=trs[("a", c)][:])
+
+        def glu_tr(k, pool):
+            c = k % 4
+            pt = bank_for_transposes(pool)
+            trs[("g", k)] = pt
+            for i in range(4):
+                nc.tensor.transpose(pt[:, i, :], gs[k // 2 * 2][:, c % 2, P * i : P * i + P], ident_f[:])
+
+        def merge(k):
+            c = k % 4
+            res = work.tile([P, 4, P], F32, name="res")
+            nc.vector.tensor_tensor(out=res[:], in0=trs[("g", k)][:], in1=acc_t[:, :, P * c : P * c + P], op=ALU.max)
+            nc.sync.dma_start(
+                out=out[0, 1].rearrange("(p i) c -> p i c", i=4)[:, :, P * c : P * c + P], in_=res[:]
+            )
+
         agg_tr(0, 0)
         agg_tr(0, 1)
         agg_ev(0, 0, "V")
-        agg_ev(0, 1, "V")
-        agg_q(0)
+        bt = psum_tr.tile([P, P], BF16, name="bt", tag="tr")
+        nc.tensor.transpose(bt[:], braw[:], ident_b[:])
         regroup(0, "r0")
         regroup(0, "l0")
-        regroup(0, "r1")
+        agg_ev(0, 1, "V")
+        agg_q(0)
+        nc.vector.tensor_copy(out=bias[:], in_=bt[:, 0 : UNITS * 8])
         quant(0, "r0")
-        regroup(0, "g2")
         quant(0, "l0")
         passr(0)
         passr(1)
         passl(0)
         passl(1)
+        regroup(0, "r1")
+        regroup(0, "g2")
         sig(0)
         sig(1)
         quant(0, "r1")
@@ -261,7 +288,6 @@ def tile_stsindividuallayer_pb_kernel(tc, agg, W, b, out):
 
         for d in range(PAIRS):
             u_next = d // 2 + 1
-            fine = d >= PAIRS - 1
             if d == 2:
                 agg_tr(1, 0)
                 agg_tr(1, 1)
@@ -270,25 +296,33 @@ def tile_stsindividuallayer_pb_kernel(tc, agg, W, b, out):
                 out_tr(9 + 2 * LATE.index(d))
             sig(2 * d + 2)
             sig(2 * d + 3)
-            if not fine:
+            if d < PAIRS - 2:
                 stt(2 * d)
                 stt(2 * d + 1)
                 max_pair(d - 1)
+            elif d == PAIRS - 2:
+                acc_tr(0, "tr")
+                acc_tr(1, "tr")
+                stt(20)
+                stt(21)
+                max_pair(d - 1)
+                acc_ev(0)
+                acc_ev(1)
+                glu_tr(20, "r")
+                acc_tr(2, "r")
             else:
-                stt(2 * d)
-                max_one(2 * d - 2)
-                out_tr(2 * d - 2)
-                stt(2 * d + 1)
-                max_one(2 * d - 1)
-                out_ev(2 * d - 2)
-                out_tr(2 * d - 1)
-                max_one(2 * d)
-                out_ev(2 * d - 1)
-                out_tr(2 * d)
-                max_one(2 * d + 1)
-                out_ev(2 * d)
-                out_tr(2 * d + 1)
-                out_ev(2 * d + 1)
+                stt(22)
+                acc_ev(2)
+                glu_tr(21, "tr")
+                acc_tr(3, "tr")
+                merge(20)
+                stt(23)
+                acc_ev(3)
+                glu_tr(22, "r")
+                merge(21)
+                glu_tr(23, "r")
+                merge(22)
+                merge(23)
             if d == 2:
                 agg_ev(1, 0, "S")
                 agg_ev(1, 1, "S")

@@ -75,8 +75,7 @@ def tile_stsindividuallayer_pb_kernel(tc, agg, W, b, out):
         load_w(0, 0, 256)
         load_w(0, 768, 1024)
         load_w(0, 256, 512)
-        load_w(1, 0, CH)
-        load_w(1, CH, 2 * CH)
+        load_w(1, 0, 2 * CH)
         load_w(2, 0, 2 * CH)
         load_x(1, 0, 4)
         for u in range(3, UNITS):

@@ -218,7 +218,7 @@ def tile_stsindividuallayer_pb_kernel(tc, agg, W, b, out):
         def out_ev(k):
             u, c = divmod(k, 4)
             w = u // NF
-            res = work.tile([P, 4, P], F32, name="res")
+            res = work.tile([P, 4, P], F32, name="res", bufs=8)
             nc.scalar.copy(out=res[:], in_=trs[k][:])
             nc.sync.dma_start(
                 out=out[0, w].rearrange("(p i) c -> p i c", i=4)[:, :, P * c : P * c + P], in_=res[:]
@@ -247,7 +247,7 @@ def tile_stsindividuallayer_pb_kernel(tc, agg, W, b, out):
 
         def merge(k):
             c = k % 4
-            res = work.tile([P, 4, P], F32, name="res")
+            res = work.tile([P, 4, P], F32, name="res", bufs=8)
             nc.vector.tensor_tensor(out=res[:], in0=trs[("g", k)][:], in1=acc_t[:, :, P * c : P * c + P], op=ALU.max)
             nc.sync.dma_start(
                 out=out[0, 1].rearrange("(p i) c -> p i c", i=4)[:, :, P * c : P * c + P], in_=res[:]

@@ -22,7 +22,7 @@ PAIRS = STEPS // 2
 FLOPS = 2 * NW * NF * NODES * 512 * 2 * CH
 
 PART = {"r0": (512, 256), "r1": (768, 256), "l0": (0, 256), "g2": (256, 128), "g3": (384, 128)}
-ON_VECTOR = ((0, "l0"), (1, "r0"), (1, "r1"), (2, "l0"), (5, "l0"))
+ON_VECTOR = ((1, "r1"), (2, "l0"), (3, "l0"), (5, "l0"))
 USE_G = True
 LATE = [8, 9]
 
@@ -69,13 +69,16 @@ def tile_stsindividuallayer_pb_kernel(tc, agg, W, b, out):
         def load_x(w, i0, i1):
             nc.sync.dma_start(out=x[w][:, i0:i1, :], in_=agg[0, w].rearrange("(p i) k -> p i k", i=4)[:, i0:i1, :])
 
+        load_w(0, 512, 768)
         load_x(0, 0, 2)
         load_x(0, 2, 4)
-        load_w(0, 512, 768)
         load_w(0, 0, 256)
         load_w(0, 768, 1024)
         load_w(0, 256, 512)
-        load_w(1, 0, 2 * CH)
+        load_w(1, 512, 768)
+        load_w(1, 0, 256)
+        load_w(1, 768, 1024)
+        load_w(1, 256, 512)
         load_w(2, 0, 2 * CH)
         load_x(1, 0, 4)
         for u in range(3, UNITS):
@@ -253,24 +256,25 @@ def tile_stsindividuallayer_pb_kernel(tc, agg, W, b, out):
                 out=out[0, 1].rearrange("(p i) c -> p i c", i=4)[:, :, P * c : P * c + P], in_=res[:]
             )
 
+        regroup(0, "r0")
         agg_tr(0, 0)
         agg_tr(0, 1)
+        quant(0, "r0")
+        regroup(0, "l0")
         agg_ev(0, 0, "V")
         bt = psum_tr.tile([P, P], BF16, name="bt", tag="tr")
         nc.tensor.transpose(bt[:], braw[:], ident_b[:])
-        regroup(0, "r0")
-        regroup(0, "l0")
+        regroup(0, "r1")
+        regroup(0, "g2")
         agg_ev(0, 1, "V")
         agg_q(0)
         nc.vector.tensor_copy(out=bias[:], in_=bt[:, 0 : UNITS * 8])
-        quant(0, "r0")
         quant(0, "l0")
         passr(0)
         passr(1)
         passl(0)
         passl(1)
-        regroup(0, "r1")
-        regroup(0, "g2")
+        regroup(1, "r0")
         sig(0)
         sig(1)
         quant(0, "r1")
@@ -279,7 +283,6 @@ def tile_stsindividuallayer_pb_kernel(tc, agg, W, b, out):
         passr(2)
         passr(3)
         passl(2)
-        regroup(1, "r0")
         regroup(1, "l0")
         quant(0, "g3")
         passl(3)

@@ -22,7 +22,7 @@ PAIRS = STEPS // 2
 FLOPS = 2 * NW * NF * NODES * 512 * 2 * CH
 
 PART = {"r0": (512, 256), "r1": (768, 256), "l0": (0, 256), "g2": (256, 128), "g3": (384, 128)}
-ON_VECTOR = ((1, "r1"), (2, "l0"), (3, "l0"), (5, "l0"))
+ON_VECTOR = ((1, "r1"), (2, "l0"), (5, "l0"))
 USE_G = True
 LATE = [8, 9]
 

@@ -23,6 +23,7 @@ FLOPS = 2 * NW * NF * NODES * 512 * 2 * CH
 
 PART = {"r0": (512, 256), "r1": (768, 256), "l0": (0, 256), "g2": (256, 128), "g3": (384, 128)}
 ON_VECTOR = ((1, "r1"), (2, "l0"), (5, "l0"))
+ON_TENSOR = ((3, "r0"), (4, "r0"))
 USE_G = True
 LATE = [8, 9]
 
@@ -102,10 +103,33 @@ def tile_stsindividuallayer_pb_kernel(tc, agg, W, b, out):
                 return "G" if (USE_G and u > 0) else "V"
             return "V" if (u, name) in ON_VECTOR else "S"
 
+        def spread(u, name):
+            if (u, name) not in ON_TENSOR:
+                return
+            c0, n = PART[name]
+            pw = psum_tr.tile([P, 2, P, 4], BF16, name="pw", tag="tr")
+            trs[("w", u, name)] = pw
+            for h in range(2):
+                nc.tensor.matmul(
+                    out=pw[:, h],
+                    lhsT=ident_b[:],
+                    rhs=raw[u][:, :, c0 + P * h : c0 + P * h + P].rearrange("p t c -> p c t"),
+                    start=True,
+                    stop=True,
+                )
+
         def regroup(u, name):
             if u >= UNITS:
                 return
             c0, n = PART[name]
+            if (u, name) in ON_TENSOR:
+                gt = stage.tile([P, n, 4], BF16, name="grouped", align_bytes=64)
+                grouped[(u, name)] = gt
+                nc.scalar.copy(
+                    out=gt[:].rearrange("p c t -> p (c t)"),
+                    in_=trs[("w", u, name)][:].rearrange("p h c t -> p (h c t)"),
+                )
+                return
             if name in ("g2", "g3"):
                 gt = stage.tile([P, n, 4], BF16, name="late", bufs=1, align_bytes=64)
             else:
@@ -338,14 +362,16 @@ def tile_stsindividuallayer_pb_kernel(tc, agg, W, b, out):
                 regroup(u_next, "g3")
             else:
                 quant(u_next, "r1")
-                regroup(u_next + 1, "r0")
                 regroup(u_next + 1, "l0")
+                regroup(u_next + 1, "r0")
                 quant(u_next, "g3")
                 regroup(u_next + 1, "g2")
             passr(2 * d + 4)
             passr(2 * d + 5)
             passl(2 * d + 4)
             passl(2 * d + 5)
+            if d % 2 == 0:
+                spread(d // 2 + 2, "r0")
             if d in LATE:
                 out_ev(8 + 2 * LATE.index(d))
                 out_ev(9 + 2 * LATE.index(d))

@@ -148,8 +148,8 @@ def tile_stsindividuallayer_pb_kernel(tc, agg, W, b, out):
             else:
                 copy_on(
                     eng,
-                    gt[:].rearrange("p (c i) t -> p c t i", i=4),
-                    raw[u][:, :, c0 : c0 + n].rearrange("p t (c i) -> p c t i", i=4),
+                    gt[:].rearrange("p (c i) t -> p c t i", i=8),
+                    raw[u][:, :, c0 : c0 + n].rearrange("p t (c i) -> p c t i", i=8),
                 )
 
         def quant(u, name):

@@ -22,7 +22,7 @@ PAIRS = STEPS // 2
 FLOPS = 2 * NW * NF * NODES * 512 * 2 * CH
 
 PART = {"r0": (512, 256), "r1": (768, 256), "l0": (0, 256), "g2": (256, 128), "g3": (384, 128)}
-ON_VECTOR = ((1, "r1"), (2, "l0"), (5, "l0"))
+ON_VECTOR = ((0, "r0"), (0, "r1"), (1, "l0"), (2, "l0"), (5, "l0"))
 ON_TENSOR = ((3, "r0"), (4, "r0"))
 USE_G = True
 LATE = [8, 9]
@@ -58,8 +58,10 @@ def tile_stsindividuallayer_pb_kernel(tc, agg, W, b, out):
 
         nc.vector.memset(warm[:], 0.0)
         nc.vector.memset(braw[:], 0.0)
-        nc.scalar.dma_start(out=braw[0 : UNITS * 8, :], in_=b.rearrange("w f (c p) -> (w f c) p", p=P))
         nc.scalar.activation(out=warm[:, 1:2], in_=warm[:, 0:1], func=ACT.Sigmoid)
+        brows = b.rearrange("w f (c p) -> (w f c) p", p=P)
+        nc.scalar.dma_start(out=braw[0:32, :], in_=brows[0:32, :])
+        nc.scalar.dma_start(out=braw[32 : UNITS * 8, :], in_=brows[32 : UNITS * 8, :])
         make_identity(nc, ident_f[:])
         make_identity(nc, ident_b[:])
 
@@ -70,9 +72,9 @@ def tile_stsindividuallayer_pb_kernel(tc, agg, W, b, out):
         def load_x(w, i0, i1):
             nc.sync.dma_start(out=x[w][:, i0:i1, :], in_=agg[0, w].rearrange("(p i) k -> p i k", i=4)[:, i0:i1, :])
 
-        load_w(0, 512, 768)
         load_x(0, 0, 2)
         load_x(0, 2, 4)
+        load_w(0, 512, 768)
         load_w(0, 0, 256)
         load_w(0, 768, 1024)
         load_w(0, 256, 512)
@@ -280,32 +282,32 @@ def tile_stsindividuallayer_pb_kernel(tc, agg, W, b, out):
                 out=out[0, 1].rearrange("(p i) c -> p i c", i=4)[:, :, P * c : P * c + P], in_=res[:]
             )
 
-        regroup(0, "r0")
         agg_tr(0, 0)
         agg_tr(0, 1)
+        agg_ev(0, 0, "S")
+        agg_ev(0, 1, "S")
+        regroup(0, "r0")
         quant(0, "r0")
-        regroup(0, "l0")
-        agg_ev(0, 0, "V")
+        agg_q(0)
         bt = psum_tr.tile([P, P], BF16, name="bt", tag="tr")
         nc.tensor.transpose(bt[:], braw[:], ident_b[:])
-        regroup(0, "r1")
-        regroup(0, "g2")
-        agg_ev(0, 1, "V")
-        agg_q(0)
         nc.vector.tensor_copy(out=bias[:], in_=bt[:, 0 : UNITS * 8])
-        quant(0, "l0")
+        regroup(0, "l0")
         passr(0)
         passr(1)
-        passl(0)
-        passl(1)
-        regroup(1, "r0")
+        regroup(0, "r1")
+        quant(0, "l0")
+        quant(0, "r1")
         sig(0)
         sig(1)
-        quant(0, "r1")
-        quant(0, "g2")
-        regroup(0, "g3")
+        passl(0)
+        passl(1)
         passr(2)
         passr(3)
+        regroup(1, "r0")
+        regroup(0, "g2")
+        quant(0, "g2")
+        regroup(0, "g3")
         passl(2)
         regroup(1, "l0")
         quant(0, "g3")

@@ -72,9 +72,11 @@ def tile_stsindividuallayer_pb_kernel(tc, agg, W, b, out):
         def load_x(w, i0, i1):
             nc.sync.dma_start(out=x[w][:, i0:i1, :], in_=agg[0, w].rearrange("(p i) k -> p i k", i=4)[:, i0:i1, :])
 
-        load_x(0, 0, 2)
-        load_x(0, 2, 4)
+        load_x(0, 0, 1)
+        load_x(0, 1, 2)
         load_w(0, 512, 768)
+        load_x(0, 2, 3)
+        load_x(0, 3, 4)
         load_w(0, 0, 256)
         load_w(0, 768, 1024)
         load_w(0, 256, 512)
@@ -179,6 +181,24 @@ def tile_stsindividuallayer_pb_kernel(tc, agg, W, b, out):
         def agg_q(w):
             nc.vector.quantize_mx(out=xcodes[w][:].bitcast(FP8X4), scales=xscales[w][:], in_=xg[w][:])
 
+        def agg_tr1(i):
+            pt = bank_for_transposes("tr" if i < 2 else "r")
+            trs[("x1", i)] = pt
+            words = x[0][:, i, :].bitcast(F32).rearrange("p (m s) -> p s m", s=2)
+            for s in range(2):
+                nc.tensor.transpose(pt[:, s, :], words[:, s, :], ident_f[:])
+
+        def agg_ev1(i, eng):
+            dst = xg[0][:].bitcast(F32).rearrange("p (r s) -> p r s", s=2)[:, P * i : P * i + P, :]
+            copy_on(eng, dst, trs[("x1", i)][:, 0:2, :].rearrange("p s r -> p r s"))
+
+        def agg_q1(h):
+            nc.vector.quantize_mx(
+                out=xcodes[0][:, 256 * h : 256 * h + 256].bitcast(FP8X4),
+                scales=xscales[0][:, 256 * h : 256 * h + 256],
+                in_=xg[0][:, 1024 * h : 1024 * h + 1024],
+            )
+
         def one_pass(bank, u, c0):
             w = u // NF
             nc.tensor.matmul_mx(
@@ -282,13 +302,13 @@ def tile_stsindividuallayer_pb_kernel(tc, agg, W, b, out):
                 out=out[0, 1].rearrange("(p i) c -> p i c", i=4)[:, :, P * c : P * c + P], in_=res[:]
             )
 
-        agg_tr(0, 0)
-        agg_tr(0, 1)
-        agg_ev(0, 0, "S")
-        agg_ev(0, 1, "S")
+        for i in range(4):
+            agg_tr1(i)
+            agg_ev1(i, "S")
         regroup(0, "r0")
         quant(0, "r0")
-        agg_q(0)
+        agg_q1(0)
+        agg_q1(1)
         bt = psum_tr.tile([P, P], BF16, name="bt", tag="tr")
         nc.tensor.transpose(bt[:], braw[:], ident_b[:])
         nc.vector.tensor_copy(out=bias[:], in_=bt[:, 0 : UNITS * 8])

from contextlib import ExitStack

import concourse.mybir as mybir
from concourse.masks import make_identity

F32 = mybir.dt.float32
BF16 = mybir.dt.bfloat16
U32 = mybir.dt.uint32
U8 = mybir.dt.uint8
FP8X4 = mybir.dt.float8_e4m3fn_x4
ACT = mybir.ActivationFunctionType
ALU = mybir.AluOpType

P = 128
NW = 2
NF = 3
NODES = 512
CH = 512
UNITS = NW * NF
STEPS = UNITS * 4
PAIRS = STEPS // 2
FLOPS = 2 * NW * NF * NODES * 512 * 2 * CH

PART = {"r0": (512, 256), "r1": (768, 256), "l0": (0, 256), "g2": (256, 128), "g3": (384, 128)}
ON_VECTOR = ((0, "r0"), (0, "r1"), (1, "l0"), (2, "l0"), (5, "l0"))
ON_TENSOR = ((3, "r0"), (4, "r0"))
USE_G = True
LATE = [8, 9]


def tile_stsindividuallayer_pb_kernel(tc, agg, W, b, out):
    nc = tc.nc
    with ExitStack() as ctx:
        const = ctx.enter_context(tc.tile_pool(name="const", bufs=1))
        keep = ctx.enter_context(tc.tile_pool(name="keep", bufs=1))
        stage = ctx.enter_context(tc.tile_pool(name="stage", bufs=6))
        work = ctx.enter_context(tc.tile_pool(name="work", bufs=3))
        psum_l = ctx.enter_context(tc.psum_pool(name="psum_l", bufs=4))
        psum_r = ctx.enter_context(tc.psum_pool(name="psum_r", bufs=2))
        psum_tr = ctx.enter_context(tc.psum_pool(name="psum_tr", bufs=2))
        ctx.enter_context(tc.manual_schedule())

        raw = [keep.tile([P, 4, 2 * CH], BF16, name="raw%d" % u) for u in range(UNITS)]
        wcodes = [keep.tile([P, 2 * CH], U32, name="wcodes%d" % u, align_bytes=64) for u in range(UNITS)]
        wscales = [keep.tile([P, 2 * CH], U8, name="wscales%d" % u, align_bytes=64) for u in range(UNITS)]
        x = [keep.tile([P, 4, 512], BF16, name="x%d" % w) for w in range(NW)]
        xg = [keep.tile([P, 4 * NODES], BF16, name="xg%d" % w, align_bytes=64) for w in range(NW)]
        xcodes = [keep.tile([P, NODES], U32, name="xcodes%d" % w, align_bytes=64) for w in range(NW)]
        xscales = [keep.tile([P, NODES], U8, name="xscales%d" % w, align_bytes=64) for w in range(NW)]
        acc = [keep.tile([P, 4, NODES], F32, name="acc%d" % w) for w in range(NW)]
        acc_t = keep.tile([P, 4, CH], F32, name="acc_t")

        ident_f = const.tile([P, P], F32, name="ident_f")
        ident_b = const.tile([P, P], BF16, name="ident_b")
        braw = const.tile([P, P], BF16, name="braw")
        bias = const.tile([P, UNITS * 8], F32, name="bias")
        warm = const.tile([P, 2], F32, name="warm")

        nc.vector.memset(warm[:], 0.0)
        nc.vector.memset(braw[:], 0.0)
        nc.scalar.activation(out=warm[:, 1:2], in_=warm[:, 0:1], func=ACT.Sigmoid)
        brows = b.rearrange("w f (c p) -> (w f c) p", p=P)
        nc.scalar.dma_start(out=braw[0:32, :], in_=brows[0:32, :])
        nc.scalar.dma_start(out=braw[32 : UNITS * 8, :], in_=brows[32 : UNITS * 8, :])
        make_identity(nc, ident_f[:])
        make_identity(nc, ident_b[:])

        def load_w(u, c0, c1):
            view = W[u // NF, u % NF].rearrange("(p j) n -> p j n", j=4)
            nc.sync.dma_start(out=raw[u][:, :, c0:c1], in_=view[:, :, c0:c1])

        def load_x(w, i0, i1):
            nc.sync.dma_start(out=x[w][:, i0:i1, :], in_=agg[0, w].rearrange("(p i) k -> p i k", i=4)[:, i0:i1, :])

        load_x(0, 0, 1)
        load_x(0, 1, 2)
        load_w(0, 512, 768)
        load_x(0, 2, 3)
        load_x(0, 3, 4)
        load_w(0, 0, 256)
        load_w(0, 768, 1024)
        load_w(0, 256, 512)
        load_w(1, 512, 768)
        load_w(1, 0, 256)
        load_w(1, 768, 1024)
        load_w(1, 256, 512)
        load_w(2, 0, 2 * CH)
        load_x(1, 0, 4)
        for u in range(3, UNITS):
            load_w(u, 0, 2 * CH)

        grouped = {}
        lbank = {}
        rbank = {}
        sigs = {}
        gs = {}
        trs = {}

        def copy_on(eng, dst, src):
            if eng == "V":
                nc.vector.tensor_copy(out=dst, in_=src)
            else:
                nc.scalar.copy(out=dst, in_=src)

        def engine_of(u, name):
            if name in ("g2", "g3"):
                return "G" if (USE_G and u > 0) else "V"
            return "V" if (u, name) in ON_VECTOR else "S"

        def spread(u, name):
            if (u, name) not in ON_TENSOR:
                return
            c0, n = PART[name]
            pw = psum_tr.tile([P, 2, P, 4], BF16, name="pw", tag="tr")
            trs[("w", u, name)] = pw
            for h in range(2):
                nc.tensor.matmul(
                    out=pw[:, h],
                    lhsT=ident_b[:],
                    rhs=raw[u][:, :, c0 + P * h : c0 + P * h + P].rearrange("p t c -> p c t"),
                    start=True,
                    stop=True,
                )

        def regroup(u, name):
            if u >= UNITS:
                return
            c0, n = PART[name]
            if (u, name) in ON_TENSOR:
                gt = stage.tile([P, n, 4], BF16, name="grouped", align_bytes=64)
                grouped[(u, name)] = gt
                nc.scalar.copy(
                    out=gt[:].rearrange("p c t -> p (c t)"),
                    in_=trs[("w", u, name)][:].rearrange("p h c t -> p (h c t)"),
                )
                return
            if name in ("g2", "g3"):
                gt = stage.tile([P, n, 4], BF16, name="late", bufs=1, align_bytes=64)
            else:
                gt = stage.tile([P, n, 4], BF16, name="grouped", align_bytes=64)
            grouped[(u, name)] = gt
            eng = engine_of(u, name)
            if eng == "G":
                nc.gpsimd.tensor_scalar(
                    out=gt[:],
                    in0=raw[u][:, :, c0 : c0 + n].rearrange("p t c -> p c t"),
                    scalar1=1.0,
                    scalar2=0.0,
                    op0=ALU.mult,
                    op1=ALU.add,
                )
            else:
                copy_on(
                    eng,
                    gt[:].rearrange("p (c i) t -> p c t i", i=8),
                    raw[u][:, :, c0 : c0 + n].rearrange("p t (c i) -> p c t i", i=8),
                )

        def quant(u, name):
            if u >= UNITS:
                return
            c0, n = PART[name]
            nc.vector.quantize_mx(
                out=wcodes[u][:, c0 : c0 + n].bitcast(FP8X4),
                scales=wscales[u][:, c0 : c0 + n],
                in_=grouped[(u, name)][:].rearrange("p c t -> p (c t)"),
            )

        def agg_tr(w, h):
            xt = psum_tr.tile([P, 2, 256], F32, name="xt", tag="tr")
            trs[("x", w, h)] = xt
            for ii in range(2):
                words = x[w][:, 2 * h + ii, :].bitcast(F32).rearrange("p (m s) -> p s m", s=2)
                for s in range(2):
                    nc.tensor.transpose(xt[:, s, P * ii : P * ii + P], words[:, s, :], ident_f[:])

        def agg_ev(w, h, eng):
            dst = xg[w][:].bitcast(F32).rearrange("p (r s) -> p r s", s=2)[:, 256 * h : 256 * h + 256, :]
            copy_on(eng, dst, trs[("x", w, h)][:].rearrange("p s r -> p r s"))

        def agg_q(w):
            nc.vector.quantize_mx(out=xcodes[w][:].bitcast(FP8X4), scales=xscales[w][:], in_=xg[w][:])

        def agg_tr1(i):
            pt = bank_for_transposes("tr" if i < 2 else "r")
            trs[("x1", i)] = pt
            words = x[0][:, i, :].bitcast(F32).rearrange("p (m s) -> p s m", s=2)
            for s in range(2):
                nc.tensor.transpose(pt[:, s, :], words[:, s, :], ident_f[:])

        def agg_ev1(i, eng):
            dst = xg[0][:].bitcast(F32).rearrange("p (r s) -> p r s", s=2)[:, P * i : P * i + P, :]
            copy_on(eng, dst, trs[("x1", i)][:, 0:2, :].rearrange("p s r -> p r s"))

        def agg_q1(h):
            nc.vector.quantize_mx(
                out=xcodes[0][:, 256 * h : 256 * h + 256].bitcast(FP8X4),
                scales=xscales[0][:, 256 * h : 256 * h + 256],
                in_=xg[0][:, 1024 * h : 1024 * h + 1024],
            )

        def one_pass(bank, u, c0):
            w = u // NF
            nc.tensor.matmul_mx(
                out=bank[:],
                lhsT=wcodes[u][:, c0 : c0 + P].bitcast(FP8X4),
                lhsT_scale=wscales[u][:, c0 : c0 + P],
                rhs=xcodes[w][:].bitcast(FP8X4),
                rhs_scale=xscales[w][:],
                start=True,
                stop=True,
            )

        def passr(k):
            if k >= STEPS:
                return
            u, c = divmod(k, 4)
            rbank[k] = psum_r.tile([P, NODES], F32, name="pr")
            one_pass(rbank[k], u, CH + P * c)

        def passl(k):
            if k >= STEPS:
                return
            u, c = divmod(k, 4)
            lbank[k] = psum_l.tile([P, NODES], F32, name="pl")
            one_pass(lbank[k], u, P * c)

        def sig(k):
            if k >= STEPS:
                return
            u, c = divmod(k, 4)
            st = work.tile([P, NODES], F32, name="sig", bufs=5)
            sigs[k] = st
            col = u * 8 + 4 + c
            nc.scalar.activation(out=st[:], in_=rbank[k][:], func=ACT.Sigmoid, bias=bias[:, col : col + 1], scale=1.0)

        def stt(k):
            u, c = divmod(k, 4)
            w, f = divmod(u, NF)
            if f == 0:
                dst = acc[w][:, c, :]
            else:
                if c % 2 == 0:
                    gs[k] = work.tile([P, 2, NODES], F32, name="glu2")
                dst = gs[k // 2 * 2][:, c % 2, :]
            col = u * 8 + c
            nc.vector.scalar_tensor_tensor(
                out=dst, in0=lbank[k][:], scalar=bias[:, col : col + 1], in1=sigs[k][:], op0=ALU.add, op1=ALU.mult
            )

        def max_pair(d):
            k = 2 * d
            u, c = divmod(k, 4)
            w, f = divmod(u, NF)
            if d >= 0 and f > 0:
                pair = acc[w][:, c : c + 2, :]
                nc.vector.tensor_tensor(out=pair, in0=pair, in1=gs[k][:], op=ALU.max)

        def out_tr(k):
            u, c = divmod(k, 4)
            w = u // NF
            pt = psum_tr.tile([P, 4, P], F32, name="pt", tag="tr")
            trs[k] = pt
            for i in range(4):
                nc.tensor.transpose(pt[:, i, :], acc[w][:, c, P * i : P * i + P], ident_f[:])

        def out_ev(k):
            u, c = divmod(k, 4)
            w = u // NF
            res = work.tile([P, 4, P], F32, name="res", bufs=8)
            nc.scalar.copy(out=res[:], in_=trs[k][:])
            nc.sync.dma_start(
                out=out[0, w].rearrange("(p i) c -> p i c", i=4)[:, :, P * c : P * c + P], in_=res[:]
            )

        def bank_for_transposes(pool):
            if pool == "tr":
                return psum_tr.tile([P, 4, P], F32, name="pt", tag="tr")
            return psum_r.tile([P, 4, P], F32, name="pr")

        def acc_tr(c, pool):
            pt = bank_for_transposes(pool)
            trs[("a", c)] = pt
            for i in range(4):
                nc.tensor.transpose(pt[:, i, :], acc[1][:, c, P * i : P * i + P], ident_f[:])

        def acc_ev(c):
            nc.scalar.copy(out=acc_t[:, :, P * c : P * c + P], in_=trs[("a", c)][:])

        def glu_tr(k, pool):
            c = k % 4
            pt = bank_for_transposes(pool)
            trs[("g", k)] = pt
            for i in range(4):
                nc.tensor.transpose(pt[:, i, :], gs[k // 2 * 2][:, c % 2, P * i : P * i + P], ident_f[:])

        def merge(k):
            c = k % 4
            res = work.tile([P, 4, P], F32, name="res", bufs=8)
            nc.vector.tensor_tensor(out=res[:], in0=trs[("g", k)][:], in1=acc_t[:, :, P * c : P * c + P], op=ALU.max)
            nc.sync.dma_start(
                out=out[0, 1].rearrange("(p i) c -> p i c", i=4)[:, :, P * c : P * c + P], in_=res[:]
            )

        for i in range(4):
            agg_tr1(i)
            agg_ev1(i, "S")
        regroup(0, "r0")
        quant(0, "r0")
        agg_q1(0)
        agg_q1(1)
        bt = psum_tr.tile([P, P], BF16, name="bt", tag="tr")
        nc.tensor.transpose(bt[:], braw[:], ident_b[:])
        nc.vector.tensor_copy(out=bias[:], in_=bt[:, 0 : UNITS * 8])
        regroup(0, "l0")
        passr(0)
        passr(1)
        regroup(0, "r1")
        quant(0, "l0")
        quant(0, "r1")
        sig(0)
        sig(1)
        passl(0)
        passl(1)
        passr(2)
        passr(3)
        regroup(1, "r0")
        regroup(0, "g2")
        quant(0, "g2")
        regroup(0, "g3")
        passl(2)
        regroup(1, "l0")
        quant(0, "g3")
        passl(3)
        regroup(1, "g2")

        for d in range(PAIRS):
            u_next = d // 2 + 1
            if d == 2:
                agg_tr(1, 0)
                agg_tr(1, 1)
            if d in LATE:
                out_tr(8 + 2 * LATE.index(d))
                out_tr(9 + 2 * LATE.index(d))
            sig(2 * d + 2)
            sig(2 * d + 3)
            if d < PAIRS - 2:
                stt(2 * d)
                stt(2 * d + 1)
                max_pair(d - 1)
            elif d == PAIRS - 2:
                acc_tr(0, "tr")
                acc_tr(1, "tr")
                stt(20)
                stt(21)
                max_pair(d - 1)
                acc_ev(0)
                acc_ev(1)
                glu_tr(20, "r")
                acc_tr(2, "r")
            else:
                stt(22)
                acc_ev(2)
                glu_tr(21, "tr")
                acc_tr(3, "tr")
                merge(20)
                stt(23)
                acc_ev(3)
                glu_tr(22, "r")
                merge(21)
                glu_tr(23, "r")
                merge(22)
                merge(23)
            if d == 2:
                agg_ev(1, 0, "S")
                agg_ev(1, 1, "S")
            if d == 3:
                agg_q(1)
            if d % 2 == 0:
                quant(u_next, "r0")
                quant(u_next, "l0")
                regroup(u_next, "r1")
                quant(u_next, "g2")
                regroup(u_next, "g3")
            else:
                quant(u_next, "r1")
                regroup(u_next + 1, "l0")
                regroup(u_next + 1, "r0")
                quant(u_next, "g3")
                regroup(u_next + 1, "g2")
            passr(2 * d + 4)
            passr(2 * d + 5)
            passl(2 * d + 4)
            passl(2 * d + 5)
            if d % 2 == 0:
                spread(d // 2 + 2, "r0")
            if d in LATE:
                out_ev(8 + 2 * LATE.index(d))
                out_ev(9 + 2 * LATE.index(d))
